import numpy as np
import ml_dtypes


def mxq(x, axis, fmt="e4m3"):
    dtype, down = {"e4m3": (ml_dtypes.float8_e4m3fn, 7), "e5m2": (ml_dtypes.float8_e5m2, 14)}[fmt]
    v = np.moveaxis(np.asarray(x, np.float32).astype(ml_dtypes.bfloat16).astype(np.float64), axis, -1)
    blocks = v.reshape(v.shape[:-1] + (-1, 32))
    amax = np.abs(blocks).max(-1, keepdims=True)
    byte = np.maximum(np.where(amax > 0, np.frexp(amax)[1] - 1 + 127, 0) - down, 1)
    scale = np.exp2(byte - 127.0)
    codes = (blocks / scale).astype(np.float32).astype(dtype).astype(np.float64)
    return np.moveaxis((codes * scale).reshape(v.shape), -1, axis)


WIDE = False


def mx_kscale(k):
    if not WIDE:
        return np.ones(k)
    levels = np.array([10, -10, 5, -5, 0])
    if k % 512:
        return np.exp2(np.random.permutation(np.resize(levels, k // 32))).repeat(32)
    a = np.empty((k // 512, 16))
    for p in range(k // 512):
        a[p, :8] = np.random.permutation(np.resize(levels, 8))
        for g in range(8):
            far = levels[np.abs(levels - a[p, g]) >= 10]
            a[p, g + 8] = far[np.random.randint(len(far))]
    return np.exp2(a.ravel()).repeat(32)


BF16 = ml_dtypes.bfloat16


def bf(x):
    return np.asarray(x, np.float32).astype(BF16)


def f64(x):
    return np.asarray(x).astype(np.float64)


B, D_IN, D_H = 512, 1024, 1024


def sigmoid(v):
    return 1.0 / (1.0 + np.exp(-v))


def draw0():
    s, t = mx_kscale(D_IN), mx_kscale(D_H)

    def w_in():
        return bf(np.random.standard_normal((D_H, D_IN)) * 0.6 / np.sqrt(D_IN) / s[None, :])

    def w_rec():
        return bf(np.random.standard_normal((D_H, D_H)) * 0.6 / np.sqrt(D_H) / t[None, :])

    def bias():
        return bf(np.random.standard_normal(D_H) * 0.3)

    return {"incoming": bf(np.random.standard_normal((B, D_IN)) * s), "h": bf(np.random.standard_normal((B, D_H)) * t),
            "W_i": w_in(), "b_W_i": bias(), "W_c": w_in(), "b_W_c": bias(),
            "U_i": w_rec(), "b_U_i": bias(), "U_c": w_rec(), "b_U_c": bias()}


def core(incoming, h, W_i, b_W_i, W_c, b_W_c, U_i, b_U_i, U_c, b_U_c):
    xq = mxq(f64(incoming), 1, "e4m3")
    hq = mxq(f64(h), 1, "e4m3")
    I = sigmoid((xq @ mxq(f64(W_i), 1, "e4m3").T) + f64(b_W_i) + (hq @ mxq(f64(U_i), 1, "e4m3").T) + f64(b_U_i))
    C_head = (xq @ mxq(f64(W_c), 1, "e4m3").T) + f64(b_W_c) + (hq @ mxq(f64(U_c), 1, "e4m3").T) + f64(b_U_c)
    return I * C_head


def e4m3fn_bytes(y):
    return np.clip(np.asarray(y, np.float64), -448.0, 448.0).astype(np.float32).astype(ml_dtypes.float8_e4m3fn).view(np.uint8)


def e4m3fn_values(b):
    return np.asarray(b, np.uint8).view(ml_dtypes.float8_e4m3fn).astype(np.float64)


def setup_inputs():
    d = draw0()
    x0 = np.asarray(d['W_i']).astype(np.float64)
    s = (np.max(np.abs(x0), axis=(0,), keepdims=True) / 448.0).astype(np.float32)
    out = {}
    for k, v in d.items():
        if k == 'W_i':
            out['W_i_bytes'] = e4m3fn_bytes(x0 / s.astype(np.float64))
            out['W_i_scale'] = s
        else:
            out[k] = v
    return out


def reference(incoming, h, W_i_bytes, W_i_scale, b_W_i, W_c, b_W_c, U_i, b_U_i, U_c, b_U_c):
    return core(incoming, h, e4m3fn_values(W_i_bytes) * W_i_scale.astype(np.float64), b_W_i, W_c, b_W_c, U_i, b_U_i, U_c, b_U_c)

@@ -1,0 +1,258 @@
+from contextlib import ExitStack
+
+import concourse.mybir as mybir
+from concourse.masks import make_identity
+
+B, D_IN, D_H = 512, 1024, 1024
+FLOPS = 2 * B * D_H * (D_IN + D_H) * 2
+
+F32 = mybir.dt.float32
+BF16 = mybir.dt.bfloat16
+U32 = mybir.dt.uint32
+U8 = mybir.dt.uint8
+FP8 = mybir.dt.float8_e4m3fn
+FP8X4 = mybir.dt.float8_e4m3fn_x4
+ADD = mybir.AluOpType.add
+MULT = mybir.AluOpType.mult
+SIGMOID = mybir.ActivationFunctionType.Sigmoid
+
+P = 128
+K = 1024
+PASSES = K // 512
+WORDS = K // 2
+F_TILES = D_H // P
+M_TILES = B // P
+WC, UC, UI, WI = 0, 1, 2, 3
+
+
+def tile_lstmcell_pa_kernel(
+    tc, incoming, h, W_i_bytes, W_i_scale, b_W_i, W_c, b_W_c, U_i, b_U_i, U_c, b_U_c, out
+):
+    nc = tc.nc
+    with ExitStack() as ctx:
+        keep = ctx.enter_context(tc.tile_pool(name="keep", bufs=1))
+        widened = ctx.enter_context(tc.tile_pool(name="widened", bufs=4))
+        stage_in = ctx.enter_context(tc.tile_pool(name="stage_in", bufs=3))
+        quant = ctx.enter_context(tc.tile_pool(name="quant", bufs=3))
+        epi = ctx.enter_context(tc.tile_pool(name="epi", bufs=3))
+        sorted_pool = ctx.enter_context(tc.tile_pool(name="sorted_pool", bufs=3))
+        psum_t = ctx.enter_context(tc.psum_pool(name="psum_t", bufs=5))
+        psum_m = ctx.enter_context(tc.psum_pool(name="psum_m", bufs=3))
+        ctx.enter_context(tc.manual_schedule())
+
+        scale_col = keep.tile([P, F_TILES], F32, name="scale_col")
+        nc.sync.dma_start(out=scale_col[:], in_=W_i_scale.rearrange("o (p c) -> (o p) c", c=F_TILES))
+        bias_rows = keep.tile([P, P], BF16, name="bias_rows")
+        nc.vector.memset(bias_rows[:], 0.0)
+        zero_col = keep.tile([P, 1], F32, name="zero_col")
+        nc.vector.memset(zero_col[:], 0.0)
+        ident = keep.tile([P, P], F32, name="ident")
+        make_identity(nc, ident[:])
+        ident_bf = keep.tile([P, P], BF16, name="ident_bf")
+        nc.vector.tensor_copy(out=ident_bf[:], in_=ident[:])
+        table_warm = keep.tile([P, 1], F32, name="table_warm")
+        nc.scalar.activation(out=table_warm[:], in_=zero_col[:], func=SIGMOID)
+
+        act_raw = {}
+        for name, src in (("x", incoming), ("h", h)):
+            for m in range(M_TILES):
+                t = keep.tile([P, K], BF16, name="raw_%s%d" % (name, m))
+                pieces = 2 if (name == "x" and m == 0) else 1
+                for i in range(pieces):
+                    cols = slice(i * K // pieces, (i + 1) * K // pieces)
+                    nc.sync.dma_start(out=t[:, cols], in_=src[m * P : (m + 1) * P, cols])
+                act_raw[(name, m)] = t
+        for v, vec in enumerate((b_W_i, b_W_c, b_U_i, b_U_c)):
+            nc.sync.dma_start(
+                out=bias_rows[F_TILES * v : F_TILES * (v + 1), :],
+                in_=vec.rearrange("(c p) -> c p", p=P),
+            )
+        scale_bc = keep.tile([P, K], F32, name="scale_bc")
+        wi_bytes = []
+        w_raw = {}
+        for f in range(F_TILES):
+            rows = slice(f * P, (f + 1) * P)
+            tb = keep.tile([P, K], U8, name="wi_bytes%d" % f)
+            nc.sync.dma_start(out=tb[:], in_=W_i_bytes[rows, :])
+            wi_bytes.append(tb)
+            for unit, src in ((WC, W_c), (UC, U_c), (UI, U_i)):
+                t = keep.tile([P, K], BF16, name="raw_w%d_%d" % (unit, f))
+                nc.sync.dma_start(out=t[:], in_=src[rows, :])
+                w_raw[(unit, f)] = t
+
+        def transpose_unit(src, sorted_words):
+            words = src.bitcast(F32)
+            bank = psum_t.tile([P, 4, P], F32, name="bank")
+            for g in range(PASSES):
+                for u in range(2):
+                    if sorted_words:
+                        picked = words[:, P * (2 * g + u) : P * (2 * g + u + 1)]
+                    else:
+                        picked = words[:, 256 * g + u : 256 * (g + 1) : 2]
+                    nc.tensor.transpose(bank[:, 2 * g + u, :], picked, ident[:])
+            return bank
+
+        is_sorted = set()
+
+        def sort_words(unit, f, copy):
+            t = sorted_pool.tile([P, WORDS], F32, name="sorted%d" % unit)
+            copy(
+                out=t[:].rearrange("p (g u j) -> p g u j", g=PASSES, u=2),
+                in_=w_raw[(unit, f)][:].bitcast(F32).rearrange("p (g j u) -> p g u j", g=PASSES, u=2),
+            )
+            w_raw[(unit, f)] = t
+            is_sorted.add((unit, f))
+
+        def copy_unit(copy, bank, dst):
+            copy(out=dst, in_=bank[:].rearrange("p (g u) r -> p g r u", u=2))
+
+        def quantize(grouped, codes, scales):
+            nc.vector.quantize_mx(out=codes[:].bitcast(FP8X4), scales=scales[:], in_=grouped[:])
+
+        def widen(f):
+            t = widened.tile([P, K], BF16, name="wi_bf")
+            nc.vector.tensor_tensor(
+                out=t[:], in0=wi_bytes[f][:].bitcast(FP8), in1=scale_bc[:], op=MULT
+            )
+            w_raw[(WI, f)] = t
+
+        act_q = {}
+
+        def prepare_activation(name, copies):
+            grouped = stage_in.tile([P, 4 * K], BF16, name="grouped", align_bytes=64)
+            dst = grouped[:].bitcast(F32).rearrange("p (g r u) -> p g r u", g=PASSES, u=2)
+            for m in range(M_TILES):
+                bank = transpose_unit(act_raw[(name, m)][:], False)
+                copy_unit(copies[m], bank, dst[:, :, m * P : (m + 1) * P, :])
+            codes = keep.tile([P, K], U32, name="codes_" + name, align_bytes=64)
+            scales = keep.tile([P, K], U8, name="scales_" + name, align_bytes=64)
+            act_q[name] = (codes, scales)
+            return grouped
+
+        w_grouped = {}
+        w_q = {}
+
+        def transpose_weights(f, copies):
+            grouped = stage_in.tile([P, 4 * K], BF16, name="grouped", align_bytes=64)
+            words = grouped[:].bitcast(F32)
+            for unit in range(4):
+                bank = transpose_unit(w_raw[(unit, f)][:], (unit, f) in is_sorted)
+                dst = words[:, WORDS * unit : WORDS * (unit + 1)].rearrange(
+                    "p (g r u) -> p g r u", g=PASSES, u=2
+                )
+                copy_unit(copies[unit], bank, dst)
+            w_grouped[f] = grouped
+
+        def quantize_weights(f):
+            codes = quant.tile([P, K], U32, name="w_codes", align_bytes=64)
+            scales = quant.tile([P, K], U8, name="w_scales", align_bytes=64)
+            quantize(w_grouped[f], codes, scales)
+            w_q[f] = (codes, scales)
+
+        def gate_group(f, unit_x, unit_h, tok0, n_tok):
+            acc = psum_m.tile([P, n_tok], F32, name="acc")
+            codes, scales = w_q[f]
+            steps = [(unit_x, "x", g) for g in range(PASSES)] + [
+                (unit_h, "h", g) for g in range(PASSES)
+            ]
+            for i, (unit, name, g) in enumerate(steps):
+                a_codes, a_scales = act_q[name]
+                cols = slice(256 * unit + P * g, 256 * unit + P * (g + 1))
+                toks = slice(B * g + tok0, B * g + tok0 + n_tok)
+                nc.tensor.matmul_mx(
+                    out=acc[:],
+                    lhsT=codes[:, cols].bitcast(FP8X4),
+                    lhsT_scale=scales[:, cols],
+                    rhs=a_codes[:, toks].bitcast(FP8X4),
+                    rhs_scale=a_scales[:, toks],
+                    start=(i == 0),
+                    stop=(i == len(steps) - 1),
+                )
+            return acc
+
+        prod = {}
+
+        def multiply(f, pieces):
+            acc_i = gate_group(f, WI, UI, 0, B)
+            gate = epi.tile([P, B], F32, name="gate")
+            nc.scalar.activation(
+                out=gate[:], in_=acc_i[:], func=SIGMOID, bias=bias[:, f : f + 1], scale=1.0
+            )
+            res = epi.tile([P, B], F32, name="res")
+            for i in range(pieces):
+                toks = slice(i * B // pieces, (i + 1) * B // pieces)
+                acc_c = gate_group(f, WC, UC, toks.start, B // pieces)
+                nc.vector.scalar_tensor_tensor(
+                    out=res[:, toks],
+                    in0=acc_c[:],
+                    scalar=bias[:, F_TILES + f : F_TILES + f + 1],
+                    in1=gate[:, toks],
+                    op0=ADD,
+                    op1=MULT,
+                )
+            prod[f] = res
+
+        out_view = out.rearrange("(m p) f -> p m f", p=P)
+
+        def store(f, copies, queues):
+            share = M_TILES // len(copies)
+            rows = epi.tile([P, M_TILES, P], F32, name="rows")
+            for i, copy in enumerate(copies):
+                ms = slice(i * share, (i + 1) * share)
+                bank = psum_t.tile([P, 4, P], F32, name="bank")
+                for m in range(ms.start, ms.stop):
+                    nc.tensor.transpose(bank[:, m, :], prod[f][:, m * P : (m + 1) * P], ident[:])
+                copy(out=rows[:, ms, :], in_=bank[:, ms, :])
+                queues[i].dma_start(out=out_view[:, ms, f * P : (f + 1) * P], in_=rows[:, ms, :])
+
+        s_copy = nc.scalar.copy
+        v_copy = nc.vector.tensor_copy
+
+        all_s = (s_copy, s_copy, s_copy, s_copy)
+        for half in range(2):
+            bank = psum_t.tile([P, 4, P], F32, name="bank")
+            for j in range(4):
+                c = 4 * half + j
+                nc.tensor.transpose(
+                    bank[:, j, :], scale_col[:, c : c + 1].to_broadcast([P, P]), ident[:]
+                )
+            nc.vector.tensor_copy(
+                out=scale_bc[:].rearrange("p (n c) -> p n c", c=F_TILES)[:, :, 4 * half : 4 * half + 4],
+                in_=bank[:].rearrange("p j n -> p n j"),
+            )
+        gx = prepare_activation("x", all_s)
+        quantize(gx, act_q["x"][0], act_q["x"][1])
+        gh = prepare_activation("h", all_s)
+
+        bias_ps = psum_m.tile([P, B], F32, name="acc")
+        nc.tensor.matmul(
+            out=bias_ps[:, 0 : 2 * F_TILES], lhsT=bias_rows[:], rhs=ident_bf[:, 0 : 2 * F_TILES],
+            start=True, stop=False,
+        )
+        nc.tensor.matmul(
+            out=bias_ps[:, 0 : 2 * F_TILES], lhsT=bias_rows[:],
+            rhs=ident_bf[:, 2 * F_TILES : 4 * F_TILES], start=False, stop=True,
+        )
+        bias = keep.tile([P, 2 * F_TILES], F32, name="bias")
+        nc.vector.tensor_copy(out=bias[:], in_=bias_ps[:, 0 : 2 * F_TILES])
+        quantize(gh, act_q["h"][0], act_q["h"][1])
+
+        widen(0)
+        transpose_weights(0, all_s)
+        widen(1)
+        quantize_weights(0)
+
+        for f in range(F_TILES - 1):
+            transpose_weights(f + 1, all_s)
+            if f + 2 < F_TILES:
+                widen(f + 2)
+                sort_words(WC, f + 2, v_copy)
+                sort_words(UC, f + 2, v_copy)
+                sort_words(UI, f + 2, v_copy)
+            if f >= 1:
+                store(f - 1, (s_copy,), (nc.sync,))
+            quantize_weights(f + 1)
+            multiply(f, 1)
+        multiply(F_TILES - 1, 2)
+        store(F_TILES - 2, (s_copy,), (nc.sync,))
+        store(F_TILES - 1, (v_copy, s_copy), (nc.sync, nc.scalar))

@@ -54,7 +54,10 @@ def tile_lstmcell_pa_kernel(
         nc.scalar.activation(out=table_warm[:], in_=zero_col[:], func=SIGMOID)
 
         act_raw = {}
-        for name, src in (("x", incoming), ("h", h)):
+        wi_bytes = {}
+        w_raw = {}
+
+        def load_activation(name, src):
             for m in range(M_TILES):
                 t = keep.tile([P, K], BF16, name="raw_%s%d" % (name, m))
                 pieces = 2 if (name == "x" and m == 0) else 1
@@ -62,23 +65,33 @@ def tile_lstmcell_pa_kernel(
                     cols = slice(i * K // pieces, (i + 1) * K // pieces)
                     nc.sync.dma_start(out=t[:, cols], in_=src[m * P : (m + 1) * P, cols])
                 act_raw[(name, m)] = t
+
+        def load_bytes(f):
+            tb = keep.tile([P, K], U8, name="wi_bytes%d" % f)
+            nc.sync.dma_start(out=tb[:], in_=W_i_bytes[f * P : (f + 1) * P, :])
+            wi_bytes[f] = tb
+
+        def load_bf16_units(f):
+            for unit, src in ((WC, W_c), (UC, U_c), (UI, U_i)):
+                t = keep.tile([P, K], BF16, name="raw_w%d_%d" % (unit, f))
+                nc.sync.dma_start(out=t[:], in_=src[f * P : (f + 1) * P, :])
+                w_raw[(unit, f)] = t
+
+        load_activation("x", incoming)
+        load_bytes(0)
+        load_activation("h", h)
+        load_bytes(1)
+        load_bf16_units(0)
         for v, vec in enumerate((b_W_i, b_W_c, b_U_i, b_U_c)):
             nc.sync.dma_start(
                 out=bias_rows[F_TILES * v : F_TILES * (v + 1), :],
                 in_=vec.rearrange("(c p) -> c p", p=P),
             )
+        load_bf16_units(1)
+        for f in range(2, F_TILES):
+            load_bytes(f)
+            load_bf16_units(f)
         scale_bc = keep.tile([P, K], F32, name="scale_bc")
-        wi_bytes = []
-        w_raw = {}
-        for f in range(F_TILES):
-            rows = slice(f * P, (f + 1) * P)
-            tb = keep.tile([P, K], U8, name="wi_bytes%d" % f)
-            nc.sync.dma_start(out=tb[:], in_=W_i_bytes[rows, :])
-            wi_bytes.append(tb)
-            for unit, src in ((WC, W_c), (UC, U_c), (UI, U_i)):
-                t = keep.tile([P, K], BF16, name="raw_w%d_%d" % (unit, f))
-                nc.sync.dma_start(out=t[:], in_=src[rows, :])
-                w_raw[(unit, f)] = t
 
         def transpose_unit(src, sorted_words):
             words = src.bitcast(F32)
@@ -132,16 +145,17 @@ def tile_lstmcell_pa_kernel(
         w_grouped = {}
         w_q = {}
 
-        def transpose_weights(f, copies):
-            grouped = stage_in.tile([P, 4 * K], BF16, name="grouped", align_bytes=64)
-            words = grouped[:].bitcast(F32)
-            for unit in range(4):
+        def transpose_weights(f, copies, units=(WC, UC, UI, WI)):
+            if f not in w_grouped:
+                grouped = stage_in.tile([P, 4 * K], BF16, name="grouped", align_bytes=64)
+                w_grouped[f] = grouped
+            words = w_grouped[f][:].bitcast(F32)
+            for unit in units:
                 bank = transpose_unit(w_raw[(unit, f)][:], (unit, f) in is_sorted)
                 dst = words[:, WORDS * unit : WORDS * (unit + 1)].rearrange(
                     "p (g r u) -> p g r u", g=PASSES, u=2
                 )
                 copy_unit(copies[unit], bank, dst)
-            w_grouped[f] = grouped
 
         def quantize_weights(f):
             codes = quant.tile([P, K], U32, name="w_codes", align_bytes=64)
@@ -221,8 +235,13 @@ def tile_lstmcell_pa_kernel(
                 in_=bank[:].rearrange("p j n -> p n j"),
             )
         gx = prepare_activation("x", all_s)
+        widen(0)
         quantize(gx, act_q["x"][0], act_q["x"][1])
         gh = prepare_activation("h", all_s)
+        widen(1)
+        quantize(gh, act_q["h"][0], act_q["h"][1])
+        transpose_weights(0, all_s, (WI, WC, UC, UI))
+        quantize_weights(0)
 
         bias_ps = psum_m.tile([P, B], F32, name="acc")
         nc.tensor.matmul(
@@ -235,15 +254,9 @@ def tile_lstmcell_pa_kernel(
         )
         bias = keep.tile([P, 2 * F_TILES], F32, name="bias")
         nc.vector.tensor_copy(out=bias[:], in_=bias_ps[:, 0 : 2 * F_TILES])
-        quantize(gh, act_q["h"][0], act_q["h"][1])
-
-        widen(0)
-        transpose_weights(0, all_s)
-        widen(1)
-        quantize_weights(0)
 
         for f in range(F_TILES - 1):
-            transpose_weights(f + 1, all_s)
+            transpose_weights(f + 1, all_s, (WI, WC, UC, UI) if f == 0 else (WC, UC, UI, WI))
             if f + 2 < F_TILES:
                 widen(f + 2)
                 sort_words(WC, f + 2, v_copy)

@@ -17,6 +17,7 @@ MULT = mybir.AluOpType.mult
 SIGMOID = mybir.ActivationFunctionType.Sigmoid
 
 P = 128
+Q = 32
 K = 1024
 PASSES = K // 512
 WORDS = K // 2
@@ -186,13 +187,13 @@ def tile_lstmcell_pa_kernel(
 
         prod = {}
 
-        def multiply(f, pieces):
+        def multiply(f, pieces, store_at_once):
             acc_i = gate_group(f, WI, UI, 0, B)
             gate = epi.tile([P, B], F32, name="gate")
             nc.scalar.activation(
                 out=gate[:], in_=acc_i[:], func=SIGMOID, bias=bias[:, f : f + 1], scale=1.0
             )
-            res = epi.tile([P, B], F32, name="res")
+            res = epi.tile([P, B], F32, name="res", align_bytes=64)
             for i in range(pieces):
                 toks = slice(i * B // pieces, (i + 1) * B // pieces)
                 acc_c = gate_group(f, WC, UC, toks.start, B // pieces)
@@ -204,20 +205,41 @@ def tile_lstmcell_pa_kernel(
                     op0=ADD,
                     op1=MULT,
                 )
-            prod[f] = res
+                prod[f] = res
+                if store_at_once:
+                    store(f, i, pieces, (nc.sync, nc.scalar))
 
-        out_view = out.rearrange("(m p) f -> p m f", p=P)
+        out_view = out.rearrange("(c j) f -> j c f", j=Q)
+        turned = {}
 
-        def store(f, copies, queues):
+        def store(f, piece, pieces, queues):
+            if f not in turned:
+                rows = epi.tile([P, B], F32, name="rows", align_bytes=64)
+                turned[f] = rows
+            width = B // pieces
+            toks = slice(piece * width, (piece + 1) * width)
+            nc.vector.transpose(out=turned[f][:, toks], in_=prod[f][:, toks])
+            for a in range(P // Q):
+                queues[a % len(queues)].dma_start(
+                    out=out_view[
+                        :, toks.start // Q : toks.stop // Q, f * P + Q * a : f * P + Q * (a + 1)
+                    ],
+                    in_=turned[f][Q * a : Q * (a + 1), toks].rearrange("p (c i) -> p c i", i=Q),
+                )
+
+        rows_view = out.rearrange("(m p) f -> p m f", p=P)
+
+        def store_by_tensor(f, copies, queues):
             share = M_TILES // len(copies)
-            rows = epi.tile([P, M_TILES, P], F32, name="rows")
+            rows = epi.tile([P, B], F32, name="rows", align_bytes=64)
+            blocks = rows[:].rearrange("p (m r) -> p m r", m=M_TILES)
             for i, copy in enumerate(copies):
                 ms = slice(i * share, (i + 1) * share)
                 bank = psum_t.tile([P, 4, P], F32, name="bank")
                 for m in range(ms.start, ms.stop):
                     nc.tensor.transpose(bank[:, m, :], prod[f][:, m * P : (m + 1) * P], ident[:])
-                copy(out=rows[:, ms, :], in_=bank[:, ms, :])
-                queues[i].dma_start(out=out_view[:, ms, f * P : (f + 1) * P], in_=rows[:, ms, :])
+                copy(out=blocks[:, ms, :], in_=bank[:, ms, :])
+                queues[i].dma_start(out=rows_view[:, ms, f * P : (f + 1) * P], in_=blocks[:, ms, :])
 
         s_copy = nc.scalar.copy
         v_copy = nc.vector.tensor_copy
@@ -260,12 +282,12 @@ def tile_lstmcell_pa_kernel(
             if f + 2 < F_TILES:
                 widen(f + 2)
                 sort_words(WC, f + 2, v_copy)
-                sort_words(UC, f + 2, v_copy)
-                sort_words(UI, f + 2, v_copy)
+                sort_words(UC, f + 2, s_copy)
+                sort_words(UI, f + 2, s_copy)
             if f >= 1:
-                store(f - 1, (s_copy,), (nc.sync,))
+                store(f - 1, 0, 1, (nc.sync,))
             quantize_weights(f + 1)
-            multiply(f, 1)
-        multiply(F_TILES - 1, 2)
-        store(F_TILES - 2, (s_copy,), (nc.sync,))
-        store(F_TILES - 1, (v_copy, s_copy), (nc.sync, nc.scalar))
+            multiply(f, 1, False)
+        store(F_TILES - 2, 0, 1, (nc.sync,))
+        multiply(F_TILES - 1, 2, False)
+        store_by_tensor(F_TILES - 1, (v_copy, s_copy), (nc.sync, nc.scalar))

@@ -282,7 +282,7 @@ def tile_lstmcell_pa_kernel(
             if f + 2 < F_TILES:
                 widen(f + 2)
                 sort_words(WC, f + 2, v_copy)
-                sort_words(UC, f + 2, s_copy)
+                sort_words(UC, f + 2, v_copy)
                 sort_words(UI, f + 2, s_copy)
             if f >= 1:
                 store(f - 1, 0, 1, (nc.sync,))

@@ -41,6 +41,8 @@ def tile_lstmcell_pa_kernel(
         psum_m = ctx.enter_context(tc.psum_pool(name="psum_m", bufs=3))
         ctx.enter_context(tc.manual_schedule())
 
+        warm_sb = keep.tile([P, B], BF16, name="warm_sb")
+        nc.vector.memset(warm_sb[:], 0.0)
         scale_col = keep.tile([P, F_TILES], F32, name="scale_col")
         nc.sync.dma_start(out=scale_col[:], in_=W_i_scale.rearrange("o (p c) -> (o p) c", c=F_TILES))
         bias_rows = keep.tile([P, P], BF16, name="bias_rows")
@@ -94,6 +96,14 @@ def tile_lstmcell_pa_kernel(
             load_bf16_units(f)
         scale_bc = keep.tile([P, K], F32, name="scale_bc")
 
+        warm_ps = psum_m.tile([P, B], F32, name="acc")
+
+        def keep_warm(n):
+            for i in range(n):
+                nc.tensor.matmul(
+                    out=warm_ps[:], lhsT=warm_sb[:, 0:P], rhs=warm_sb[:], start=True, stop=True
+                )
+
         def transpose_unit(src, sorted_words):
             words = src.bitcast(F32)
             bank = psum_t.tile([P, 4, P], F32, name="bank")
@@ -138,6 +148,8 @@ def tile_lstmcell_pa_kernel(
             for m in range(M_TILES):
                 bank = transpose_unit(act_raw[(name, m)][:], False)
                 copy_unit(copies[m], bank, dst[:, :, m * P : (m + 1) * P, :])
+                if m % 2 == 1:
+                    keep_warm(1)
             codes = keep.tile([P, K], U32, name="codes_" + name, align_bytes=64)
             scales = keep.tile([P, K], U8, name="scales_" + name, align_bytes=64)
             act_q[name] = (codes, scales)
@@ -146,12 +158,14 @@ def tile_lstmcell_pa_kernel(
         w_grouped = {}
         w_q = {}
 
-        def transpose_weights(f, copies, units=(WC, UC, UI, WI)):
+        def transpose_weights(f, copies, units=(WC, UC, UI, WI), warm=False):
             if f not in w_grouped:
                 grouped = stage_in.tile([P, 4 * K], BF16, name="grouped", align_bytes=64)
                 w_grouped[f] = grouped
             words = w_grouped[f][:].bitcast(F32)
-            for unit in units:
+            for i, unit in enumerate(units):
+                if warm and i == 2:
+                    keep_warm(1)
                 bank = transpose_unit(w_raw[(unit, f)][:], (unit, f) in is_sorted)
                 dst = words[:, WORDS * unit : WORDS * (unit + 1)].rearrange(
                     "p (g r u) -> p g r u", g=PASSES, u=2
@@ -245,6 +259,7 @@ def tile_lstmcell_pa_kernel(
         v_copy = nc.vector.tensor_copy
 
         all_s = (s_copy, s_copy, s_copy, s_copy)
+        keep_warm(3)
         for half in range(2):
             bank = psum_t.tile([P, 4, P], F32, name="bank")
             for j in range(4):
@@ -262,7 +277,8 @@ def tile_lstmcell_pa_kernel(
         gh = prepare_activation("h", all_s)
         widen(1)
         quantize(gh, act_q["h"][0], act_q["h"][1])
-        transpose_weights(0, all_s, (WI, WC, UC, UI))
+        transpose_weights(0, all_s, (WI, WC, UC, UI), True)
+        keep_warm(1)
         quantize_weights(0)
 
         bias_ps = psum_m.tile([P, B], F32, name="acc")
@@ -278,7 +294,7 @@ def tile_lstmcell_pa_kernel(
         nc.vector.tensor_copy(out=bias[:], in_=bias_ps[:, 0 : 2 * F_TILES])
 
         for f in range(F_TILES - 1):
-            transpose_weights(f + 1, all_s, (WI, WC, UC, UI) if f == 0 else (WC, UC, UI, WI))
+            transpose_weights(f + 1, all_s, (WI, WC, UC, UI) if f == 0 else (WC, UC, UI, WI), f == 0)
             if f + 2 < F_TILES:
                 widen(f + 2)
                 sort_words(WC, f + 2, v_copy)

@@ -178,6 +178,18 @@ def tile_lstmcell_pa_kernel(
             quantize(w_grouped[f], codes, scales)
             w_q[f] = (codes, scales)
 
+        def quantize_half(f, half):
+            if f not in w_q:
+                codes = quant.tile([P, K], U32, name="w_codes", align_bytes=64)
+                scales = quant.tile([P, K], U8, name="w_scales", align_bytes=64)
+                w_q[f] = (codes, scales)
+            codes, scales = w_q[f]
+            cols = slice(half * K // 2, (half + 1) * K // 2)
+            nc.vector.quantize_mx(
+                out=codes[:, cols].bitcast(FP8X4), scales=scales[:, cols],
+                in_=w_grouped[f][:, 4 * cols.start : 4 * cols.stop],
+            )
+
         def gate_group(f, unit_x, unit_h, tok0, n_tok):
             acc = psum_m.tile([P, n_tok], F32, name="acc")
             codes, scales = w_q[f]
@@ -294,7 +306,11 @@ def tile_lstmcell_pa_kernel(
         nc.vector.tensor_copy(out=bias[:], in_=bias_ps[:, 0 : 2 * F_TILES])
 
         for f in range(F_TILES - 1):
-            transpose_weights(f + 1, all_s, (WI, WC, UC, UI) if f == 0 else (WC, UC, UI, WI), f == 0)
+            last = f + 1 == F_TILES - 1
+            transpose_weights(
+                f + 1, all_s,
+                (WI, WC, UC, UI) if f == 0 else ((UI, WI, WC, UC) if last else (WC, UC, UI, WI)), f == 0,
+            )
             if f + 2 < F_TILES:
                 widen(f + 2)
                 sort_words(WC, f + 2, v_copy)
@@ -302,7 +318,11 @@ def tile_lstmcell_pa_kernel(
                 sort_words(UI, f + 2, s_copy)
             if f >= 1:
                 store(f - 1, 0, 1, (nc.sync,))
-            quantize_weights(f + 1)
+            if last:
+                quantize_half(f + 1, 1)
+                quantize_half(f + 1, 0)
+            else:
+                quantize_weights(f + 1)
             multiply(f, 1, False)
         store(F_TILES - 2, 0, 1, (nc.sync,))
         multiply(F_TILES - 1, 2, False)

from contextlib import ExitStack

import concourse.mybir as mybir
from concourse.masks import make_identity

B, D_IN, D_H = 512, 1024, 1024
FLOPS = 2 * B * D_H * (D_IN + D_H) * 2

F32 = mybir.dt.float32
BF16 = mybir.dt.bfloat16
U32 = mybir.dt.uint32
U8 = mybir.dt.uint8
FP8 = mybir.dt.float8_e4m3fn
FP8X4 = mybir.dt.float8_e4m3fn_x4
ADD = mybir.AluOpType.add
MULT = mybir.AluOpType.mult
SIGMOID = mybir.ActivationFunctionType.Sigmoid

P = 128
Q = 32
K = 1024
PASSES = K // 512
WORDS = K // 2
F_TILES = D_H // P
M_TILES = B // P
WC, UC, UI, WI = 0, 1, 2, 3


def tile_lstmcell_pa_kernel(
    tc, incoming, h, W_i_bytes, W_i_scale, b_W_i, W_c, b_W_c, U_i, b_U_i, U_c, b_U_c, out
):
    nc = tc.nc
    with ExitStack() as ctx:
        keep = ctx.enter_context(tc.tile_pool(name="keep", bufs=1))
        widened = ctx.enter_context(tc.tile_pool(name="widened", bufs=4))
        stage_in = ctx.enter_context(tc.tile_pool(name="stage_in", bufs=3))
        quant = ctx.enter_context(tc.tile_pool(name="quant", bufs=3))
        epi = ctx.enter_context(tc.tile_pool(name="epi", bufs=3))
        sorted_pool = ctx.enter_context(tc.tile_pool(name="sorted_pool", bufs=3))
        psum_t = ctx.enter_context(tc.psum_pool(name="psum_t", bufs=5))
        psum_m = ctx.enter_context(tc.psum_pool(name="psum_m", bufs=3))
        ctx.enter_context(tc.manual_schedule())

        warm_sb = keep.tile([P, B], BF16, name="warm_sb")
        nc.vector.memset(warm_sb[:], 0.0)
        scale_col = keep.tile([P, F_TILES], F32, name="scale_col")
        nc.sync.dma_start(out=scale_col[:], in_=W_i_scale.rearrange("o (p c) -> (o p) c", c=F_TILES))
        bias_rows = keep.tile([P, P], BF16, name="bias_rows")
        nc.vector.memset(bias_rows[:], 0.0)
        zero_col = keep.tile([P, 1], F32, name="zero_col")
        nc.vector.memset(zero_col[:], 0.0)
        ident = keep.tile([P, P], F32, name="ident")
        make_identity(nc, ident[:])
        ident_bf = keep.tile([P, P], BF16, name="ident_bf")
        nc.vector.tensor_copy(out=ident_bf[:], in_=ident[:])
        table_warm = keep.tile([P, 1], F32, name="table_warm")
        nc.scalar.activation(out=table_warm[:], in_=zero_col[:], func=SIGMOID)

        act_raw = {}
        wi_bytes = {}
        w_raw = {}

        def load_activation(name, src):
            for m in range(M_TILES):
                t = keep.tile([P, K], BF16, name="raw_%s%d" % (name, m))
                pieces = 2 if (name == "x" and m == 0) else 1
                for i in range(pieces):
                    cols = slice(i * K // pieces, (i + 1) * K // pieces)
                    nc.sync.dma_start(out=t[:, cols], in_=src[m * P : (m + 1) * P, cols])
                act_raw[(name, m)] = t

        def load_bytes(f):
            tb = keep.tile([P, K], U8, name="wi_bytes%d" % f)
            nc.sync.dma_start(out=tb[:], in_=W_i_bytes[f * P : (f + 1) * P, :])
            wi_bytes[f] = tb

        def load_bf16_units(f):
            for unit, src in ((WC, W_c), (UC, U_c), (UI, U_i)):
                t = keep.tile([P, K], BF16, name="raw_w%d_%d" % (unit, f))
                nc.sync.dma_start(out=t[:], in_=src[f * P : (f + 1) * P, :])
                w_raw[(unit, f)] = t

        load_activation("x", incoming)
        load_bytes(0)
        load_activation("h", h)
        load_bytes(1)
        load_bf16_units(0)
        for v, vec in enumerate((b_W_i, b_W_c, b_U_i, b_U_c)):
            nc.sync.dma_start(
                out=bias_rows[F_TILES * v : F_TILES * (v + 1), :],
                in_=vec.rearrange("(c p) -> c p", p=P),
            )
        load_bf16_units(1)
        for f in range(2, F_TILES):
            load_bytes(f)
            load_bf16_units(f)
        scale_bc = keep.tile([P, K], F32, name="scale_bc")

        warm_ps = psum_m.tile([P, B], F32, name="acc")

        def keep_warm(n):
            for i in range(n):
                nc.tensor.matmul(
                    out=warm_ps[:], lhsT=warm_sb[:, 0:P], rhs=warm_sb[:], start=True, stop=True
                )

        def transpose_unit(src, sorted_words):
            words = src.bitcast(F32)
            bank = psum_t.tile([P, 4, P], F32, name="bank")
            for g in range(PASSES):
                for u in range(2):
                    if sorted_words:
                        picked = words[:, P * (2 * g + u) : P * (2 * g + u + 1)]
                    else:
                        picked = words[:, 256 * g + u : 256 * (g + 1) : 2]
                    nc.tensor.transpose(bank[:, 2 * g + u, :], picked, ident[:])
            return bank

        is_sorted = set()

        def sort_words(unit, f, copy):
            t = sorted_pool.tile([P, WORDS], F32, name="sorted%d" % unit)
            copy(
                out=t[:].rearrange("p (g u j) -> p g u j", g=PASSES, u=2),
                in_=w_raw[(unit, f)][:].bitcast(F32).rearrange("p (g j u) -> p g u j", g=PASSES, u=2),
            )
            w_raw[(unit, f)] = t
            is_sorted.add((unit, f))

        def copy_unit(copy, bank, dst):
            copy(out=dst, in_=bank[:].rearrange("p (g u) r -> p g r u", u=2))

        def quantize(grouped, codes, scales):
            nc.vector.quantize_mx(out=codes[:].bitcast(FP8X4), scales=scales[:], in_=grouped[:])

        def widen(f):
            t = widened.tile([P, K], BF16, name="wi_bf")
            nc.vector.tensor_tensor(
                out=t[:], in0=wi_bytes[f][:].bitcast(FP8), in1=scale_bc[:], op=MULT
            )
            w_raw[(WI, f)] = t

        act_q = {}

        def prepare_activation(name, copies):
            grouped = stage_in.tile([P, 4 * K], BF16, name="grouped", align_bytes=64)
            dst = grouped[:].bitcast(F32).rearrange("p (g r u) -> p g r u", g=PASSES, u=2)
            for m in range(M_TILES):
                bank = transpose_unit(act_raw[(name, m)][:], False)
                copy_unit(copies[m], bank, dst[:, :, m * P : (m + 1) * P, :])
                if m % 2 == 1:
                    keep_warm(1)
            codes = keep.tile([P, K], U32, name="codes_" + name, align_bytes=64)
            scales = keep.tile([P, K], U8, name="scales_" + name, align_bytes=64)
            act_q[name] = (codes, scales)
            return grouped

        w_grouped = {}
        w_q = {}

        def transpose_weights(f, copies, units=(WC, UC, UI, WI), warm=False):
            if f not in w_grouped:
                grouped = stage_in.tile([P, 4 * K], BF16, name="grouped", align_bytes=64)
                w_grouped[f] = grouped
            words = w_grouped[f][:].bitcast(F32)
            for i, unit in enumerate(units):
                if warm and i == 2:
                    keep_warm(1)
                bank = transpose_unit(w_raw[(unit, f)][:], (unit, f) in is_sorted)
                dst = words[:, WORDS * unit : WORDS * (unit + 1)].rearrange(
                    "p (g r u) -> p g r u", g=PASSES, u=2
                )
                copy_unit(copies[unit], bank, dst)

        def quantize_weights(f):
            codes = quant.tile([P, K], U32, name="w_codes", align_bytes=64)
            scales = quant.tile([P, K], U8, name="w_scales", align_bytes=64)
            quantize(w_grouped[f], codes, scales)
            w_q[f] = (codes, scales)

        def quantize_half(f, half):
            if f not in w_q:
                codes = quant.tile([P, K], U32, name="w_codes", align_bytes=64)
                scales = quant.tile([P, K], U8, name="w_scales", align_bytes=64)
                w_q[f] = (codes, scales)
            codes, scales = w_q[f]
            cols = slice(half * K // 2, (half + 1) * K // 2)
            nc.vector.quantize_mx(
                out=codes[:, cols].bitcast(FP8X4), scales=scales[:, cols],
                in_=w_grouped[f][:, 4 * cols.start : 4 * cols.stop],
            )

        def gate_group(f, unit_x, unit_h, tok0, n_tok):
            acc = psum_m.tile([P, n_tok], F32, name="acc")
            codes, scales = w_q[f]
            steps = [(unit_x, "x", g) for g in range(PASSES)] + [
                (unit_h, "h", g) for g in range(PASSES)
            ]
            for i, (unit, name, g) in enumerate(steps):
                a_codes, a_scales = act_q[name]
                cols = slice(256 * unit + P * g, 256 * unit + P * (g + 1))
                toks = slice(B * g + tok0, B * g + tok0 + n_tok)
                nc.tensor.matmul_mx(
                    out=acc[:],
                    lhsT=codes[:, cols].bitcast(FP8X4),
                    lhsT_scale=scales[:, cols],
                    rhs=a_codes[:, toks].bitcast(FP8X4),
                    rhs_scale=a_scales[:, toks],
                    start=(i == 0),
                    stop=(i == len(steps) - 1),
                )
            return acc

        prod = {}

        def multiply(f, pieces, store_at_once):
            acc_i = gate_group(f, WI, UI, 0, B)
            gate = epi.tile([P, B], F32, name="gate")
            nc.scalar.activation(
                out=gate[:], in_=acc_i[:], func=SIGMOID, bias=bias[:, f : f + 1], scale=1.0
            )
            res = epi.tile([P, B], F32, name="res", align_bytes=64)
            for i in range(pieces):
                toks = slice(i * B // pieces, (i + 1) * B // pieces)
                acc_c = gate_group(f, WC, UC, toks.start, B // pieces)
                nc.vector.scalar_tensor_tensor(
                    out=res[:, toks],
                    in0=acc_c[:],
                    scalar=bias[:, F_TILES + f : F_TILES + f + 1],
                    in1=gate[:, toks],
                    op0=ADD,
                    op1=MULT,
                )
                prod[f] = res
                if store_at_once:
                    store(f, i, pieces, (nc.sync, nc.scalar))

        out_view = out.rearrange("(c j) f -> j c f", j=Q)
        turned = {}

        def store(f, piece, pieces, queues):
            if f not in turned:
                rows = epi.tile([P, B], F32, name="rows", align_bytes=64)
                turned[f] = rows
            width = B // pieces
            toks = slice(piece * width, (piece + 1) * width)
            nc.vector.transpose(out=turned[f][:, toks], in_=prod[f][:, toks])
            for a in range(P // Q):
                queues[a % len(queues)].dma_start(
                    out=out_view[
                        :, toks.start // Q : toks.stop // Q, f * P + Q * a : f * P + Q * (a + 1)
                    ],
                    in_=turned[f][Q * a : Q * (a + 1), toks].rearrange("p (c i) -> p c i", i=Q),
                )

        rows_view = out.rearrange("(m p) f -> p m f", p=P)

        def store_by_tensor(f, copies, queues):
            share = M_TILES // len(copies)
            rows = epi.tile([P, B], F32, name="rows", align_bytes=64)
            blocks = rows[:].rearrange("p (m r) -> p m r", m=M_TILES)
            for i, copy in enumerate(copies):
                ms = slice(i * share, (i + 1) * share)
                bank = psum_t.tile([P, 4, P], F32, name="bank")
                for m in range(ms.start, ms.stop):
                    nc.tensor.transpose(bank[:, m, :], prod[f][:, m * P : (m + 1) * P], ident[:])
                copy(out=blocks[:, ms, :], in_=bank[:, ms, :])
                queues[i].dma_start(out=rows_view[:, ms, f * P : (f + 1) * P], in_=blocks[:, ms, :])

        s_copy = nc.scalar.copy
        v_copy = nc.vector.tensor_copy

        all_s = (s_copy, s_copy, s_copy, s_copy)
        keep_warm(3)
        for half in range(2):
            bank = psum_t.tile([P, 4, P], F32, name="bank")
            for j in range(4):
                c = 4 * half + j
                nc.tensor.transpose(
                    bank[:, j, :], scale_col[:, c : c + 1].to_broadcast([P, P]), ident[:]
                )
            nc.vector.tensor_copy(
                out=scale_bc[:].rearrange("p (n c) -> p n c", c=F_TILES)[:, :, 4 * half : 4 * half + 4],
                in_=bank[:].rearrange("p j n -> p n j"),
            )
        gx = prepare_activation("x", all_s)
        widen(0)
        quantize(gx, act_q["x"][0], act_q["x"][1])
        gh = prepare_activation("h", all_s)
        widen(1)
        quantize(gh, act_q["h"][0], act_q["h"][1])
        transpose_weights(0, all_s, (WI, WC, UC, UI), True)
        keep_warm(1)
        quantize_weights(0)

        bias_ps = psum_m.tile([P, B], F32, name="acc")
        nc.tensor.matmul(
            out=bias_ps[:, 0 : 2 * F_TILES], lhsT=bias_rows[:], rhs=ident_bf[:, 0 : 2 * F_TILES],
            start=True, stop=False,
        )
        nc.tensor.matmul(
            out=bias_ps[:, 0 : 2 * F_TILES], lhsT=bias_rows[:],
            rhs=ident_bf[:, 2 * F_TILES : 4 * F_TILES], start=False, stop=True,
        )
        bias = keep.tile([P, 2 * F_TILES], F32, name="bias")
        nc.vector.tensor_copy(out=bias[:], in_=bias_ps[:, 0 : 2 * F_TILES])

        for f in range(F_TILES - 1):
            last = f + 1 == F_TILES - 1
            transpose_weights(
                f + 1, all_s,
                (WI, WC, UC, UI) if f == 0 else ((UI, WI, WC, UC) if last else (WC, UC, UI, WI)), f == 0,
            )
            if f + 2 < F_TILES:
                widen(f + 2)
                sort_words(WC, f + 2, v_copy)
                sort_words(UC, f + 2, v_copy)
                sort_words(UI, f + 2, s_copy)
            if f >= 1:
                store(f - 1, 0, 1, (nc.sync,))
            if last:
                quantize_half(f + 1, 1)
                quantize_half(f + 1, 0)
            else:
                quantize_weights(f + 1)
            multiply(f, 1, False)
        store(F_TILES - 2, 0, 1, (nc.sync,))
        multiply(F_TILES - 1, 2, False)
        store_by_tensor(F_TILES - 1, (v_copy, s_copy), (nc.sync, nc.scalar))
